import numpy as np
import ml_dtypes


def mxq(x, axis, fmt="e4m3"):
    dtype, down = {"e4m3": (ml_dtypes.float8_e4m3fn, 7), "e5m2": (ml_dtypes.float8_e5m2, 14)}[fmt]
    v = np.moveaxis(np.asarray(x, np.float32).astype(ml_dtypes.bfloat16).astype(np.float64), axis, -1)
    blocks = v.reshape(v.shape[:-1] + (-1, 32))
    amax = np.abs(blocks).max(-1, keepdims=True)
    byte = np.maximum(np.where(amax > 0, np.frexp(amax)[1] - 1 + 127, 0) - down, 1)
    scale = np.exp2(byte - 127.0)
    codes = (blocks / scale).astype(np.float32).astype(dtype).astype(np.float64)
    return np.moveaxis((codes * scale).reshape(v.shape), -1, axis)


WIDE = False


def mx_kscale(k):
    if not WIDE:
        return np.ones(k)
    levels = np.array([10, -10, 5, -5, 0])
    a = np.random.permutation(np.resize(levels, k // 512 * 4)).reshape(k // 512, 4)
    idx = np.arange(k)
    return np.exp2(a[idx // 512, idx % 128 // 32])


BF16 = ml_dtypes.bfloat16


def bf(x):
    return np.asarray(x, np.float32).astype(BF16)


def f64(x):
    return np.asarray(x).astype(np.float64)


R, D, B, T = 128, 1024, 4, 2048


def setup_inputs():
    s = mx_kscale(D)
    sigma_base = np.sqrt((np.sum(s * s) + 0.3 * np.sum(1.0 / (s * s))) / 20.8)
    return {"z": bf(np.random.standard_normal((B, T, D)) * s),
            "mu": bf((np.random.random((R, D)) * 1.9 - 0.95) / s),
            "K": bf(np.random.standard_normal((R, D)) * 0.5 / np.sqrt(D) / s),
            "log_sigma": bf(np.log(sigma_base) + 0.03 * np.random.standard_normal(R)),
            "phi": bf(np.random.random(R) * 2.0 * np.pi)}


def reference(z, mu, K, log_sigma, phi):
    z, mu, K = f64(z), f64(mu), f64(K)
    sigma_sq = np.exp(f64(log_sigma)) ** 2 + 1e-8
    z_sq = np.sum(z * z, axis=-1, keepdims=True)
    mu_sq = np.sum(mu * mu, axis=-1)
    zq = mxq(z, 2, "e4m3")
    cross = zq @ mxq(mu, 1, "e4m3").T
    D_sq = np.maximum(z_sq + mu_sq - 2.0 * cross, 0.0)
    window = np.exp(-D_sq / (2.0 * sigma_sq))
    window = window / np.maximum(np.sum(window, axis=-1, keepdims=True), 1e-6)
    phase = (zq @ mxq(K, 1, "e4m3").T) + f64(phi)
    return window * np.cos(phase)

@@ -1,0 +1,320 @@
+import math
+from contextlib import ExitStack
+
+import concourse.mybir as mybir
+from concourse.masks import make_identity
+
+F32 = mybir.dt.float32
+BF16 = mybir.dt.bfloat16
+I32 = mybir.dt.int32
+U32 = mybir.dt.uint32
+U8 = mybir.dt.uint8
+FP8X4 = mybir.dt.float8_e4m3fn_x4
+ALU = mybir.AluOpType
+ACT = mybir.ActivationFunctionType
+
+P = 128
+R = 128
+D = 1024
+TOKENS = 8192
+J = 4
+GT = P * J
+NG = TOKENS // GT
+NZ = 5
+NXT = 4
+S_EXIT_GROUPS = (2, 4, 6, 8, 10, 12, 14, 15)
+
+FLOPS = 2 * 2 * TOKENS * R * D
+
+SQRT_HALF = math.sqrt(0.5)
+TWO_PI = 2.0 * math.pi
+INV_TWO_PI = 1.0 / TWO_PI
+HALF_PI = 0.5 * math.pi
+
+
+def tile_gaborbasis_t_kernel(tc, z, mu, K, log_sigma, phi, out):
+    nc = tc.nc
+    z_groups = z.flatten_outer_dims().rearrange("(g p j) k -> g p j k", p=P, j=J)
+    o_groups = out.flatten_outer_dims().rearrange("(g p j) r -> g p (j r)", p=P, j=J)
+
+    with ExitStack() as ctx:
+        ctx.enter_context(tc.manual_schedule())
+        const = ctx.enter_context(tc.tile_pool(name="const", bufs=1))
+        zpool = ctx.enter_context(tc.tile_pool(name="zpool", bufs=NZ))
+        work = ctx.enter_context(tc.tile_pool(name="work", bufs=2))
+        vpool = ctx.enter_context(tc.tile_pool(name="vpool", bufs=3))
+        psum = ctx.enter_context(tc.psum_pool(name="psum", bufs=1))
+
+        z_tiles = {}
+        xt_tiles = {}
+        grp_tiles = {}
+        q_tiles = {}
+        xy_tiles = {}
+        v_tiles = {}
+
+        def new_z(g):
+            z_tiles[g] = zpool.tile([P, J * D], BF16, name="z_sb")
+
+        def load(g):
+            new_z(g)
+            nc.sync.dma_start(out=z_tiles[g][:].rearrange("p (j k) -> p j k", j=J), in_=z_groups[g])
+
+        def load_part(g, j):
+            nc.sync.dma_start(out=z_tiles[g][:, j * D : (j + 1) * D], in_=z_groups[g][:, j, :])
+
+        rows = const.tile([P, 2 * R], BF16, name="rows")
+        nc.vector.memset(rows[:], 0.0)
+        wk = const.tile([P, 2 * D], BF16, name="wk")
+        new_z(0)
+        load_part(0, 0)
+        nc.sync.dma_start(out=rows[0:1, 0:R], in_=log_sigma.unsqueeze(0))
+        nc.sync.dma_start(out=rows[0:1, R : 2 * R], in_=phi.unsqueeze(0))
+        nc.sync.dma_start(out=wk[:, 0:D], in_=mu)
+        nc.sync.dma_start(out=wk[:, D : 2 * D], in_=K)
+        for j in range(1, J):
+            load_part(0, j)
+        for g in range(1, NZ):
+            load(g)
+
+        ones_bf = const.tile([P, P], BF16, name="ones_bf")
+        nc.vector.memset(ones_bf[:], 1.0)
+        warm = const.tile([P, 2], F32, name="warm")
+        nc.vector.memset(warm[:], 0.0)
+        nc.scalar.activation(out=warm[:, 1:2], in_=warm[:, 0:1], func=ACT.Exp)
+        ident = const.tile([P, P], F32, name="ident")
+        make_identity(nc, ident[:])
+
+        zh = const.tile([P, NG * J], F32, name="zh")
+        ssum = const.tile([P, NG * J], F32, name="ssum")
+        rs = const.tile([P, NG * J], F32, name="rs")
+        f_all = const.tile([P, TOKENS], F32, name="f_all")
+        e_all = const.tile([P, TOKENS], F32, name="e_all")
+
+        def sq_tile(g, j):
+            junk = work.tile([P, D], BF16, name="junk")
+            nc.scalar.activation(
+                out=junk[:],
+                in_=z_tiles[g][:, j * D : (j + 1) * D],
+                func=ACT.Square,
+                scale=SQRT_HALF,
+                accum_out=zh[:, g * J + j : g * J + j + 1],
+            )
+
+        def sq(g):
+            for j in range(J):
+                sq_tile(g, j)
+
+        def tr_tile(g, j):
+            z_w = z_tiles[g][:].bitcast(F32)
+            t = g * J + j
+            xt = psum.tile([P, 512], F32, name="xt", tag="xt%d" % (t % NXT))
+            for cu in range(4):
+                nc.tensor.transpose(
+                    xt[:, cu * P : (cu + 1) * P], z_w[:, j * 512 + cu * P : j * 512 + (cu + 1) * P], ident[:]
+                )
+            xt_tiles[t] = xt
+
+        def new_grp(g):
+            grp_tiles[g] = work.tile([P, J * D], BF16, name="grp", align_bytes=64)
+
+        def exit_tile(g, j, on_scalar):
+            grp_w = grp_tiles[g][:].bitcast(F32).rearrange("p (j c t u) -> p j c t u", j=J, c=2, u=2)
+            src = xt_tiles[g * J + j][:].rearrange("p (c u t) -> p c t u", c=2, u=2)
+            if on_scalar:
+                nc.scalar.copy(out=grp_w[:, j, :, :, :], in_=src)
+            else:
+                nc.vector.tensor_copy(out=grp_w[:, j, :, :, :], in_=src)
+
+        def quant(g):
+            codes = work.tile([P, J * 2 * P], U32, name="codes", align_bytes=64)
+            scales = work.tile([P, J * 2 * P], U8, name="scales", align_bytes=64)
+            nc.vector.quantize_mx(out=codes[:].bitcast(FP8X4), scales=scales[:], in_=grp_tiles[g][:])
+            q_tiles[g] = (codes, scales)
+
+        new_grp(0)
+        tr_tile(0, 0)
+        sq_tile(0, 0)
+        exit_tile(0, 0, False)
+
+        pb = psum.tile([P, 512], F32, name="pb", tag="x0")
+        nc.tensor.matmul(pb[:, 0 : 2 * R], lhsT=ones_bf[:], rhs=rows[:], start=True, stop=True)
+        bc = const.tile([P, 2 * R], F32, name="bc")
+        nc.vector.tensor_copy(out=bc[:], in_=pb[:, 0 : 2 * R])
+        inv_sig = const.tile([P, R], F32, name="inv_sig")
+        nc.scalar.activation(out=inv_sig[:], in_=bc[:, 0:R], func=ACT.Exp, scale=2.0)
+        phi2 = const.tile([P, R], F32, name="phi2")
+        nc.vector.tensor_scalar(
+            out=phi2[:], in0=bc[:, R : 2 * R], scalar1=HALF_PI, scalar2=INV_TWO_PI, op0=ALU.add, op1=ALU.mult
+        )
+
+        wk_w = wk[:].bitcast(F32)
+        gwk = const.tile([P, 2 * 2 * R * 4], BF16, name="gwk", align_bytes=64)
+        gwk_w = gwk[:].bitcast(F32).rearrange("p (c w r u) -> p c w r u", c=2, w=2, u=2)
+        for w in range(2):
+            wt = psum.tile([P, 512], F32, name="wt", tag="xt%d" % (2 + w))
+            for cu in range(4):
+                nc.tensor.transpose(
+                    wt[:, cu * P : (cu + 1) * P], wk_w[:, w * 512 + cu * P : w * 512 + (cu + 1) * P], ident[:]
+                )
+            nc.vector.tensor_copy(
+                out=gwk_w[:, :, w, :, :], in_=wt[:].rearrange("p (c u r) -> p c r u", c=2, u=2)
+            )
+        w_codes = const.tile([P, 4 * R], U32, name="w_codes", align_bytes=64)
+        w_scales = const.tile([P, 4 * R], U8, name="w_scales", align_bytes=64)
+
+        junk0 = work.tile([P, D], BF16, name="junk")
+        muh_col = const.tile([P, 1], F32, name="muh_col")
+        nc.scalar.activation(
+            out=junk0[:], in_=wk[:, 0:D], func=ACT.Square, scale=SQRT_HALF, accum_out=muh_col[:]
+        )
+        nc.vector.tensor_scalar_add(out=inv_sig[:], in0=inv_sig[:], scalar1=1e-8)
+        nc.vector.reciprocal(out=inv_sig[:], in_=inv_sig[:])
+        nc.vector.quantize_mx(out=w_codes[:].bitcast(FP8X4), scales=w_scales[:], in_=gwk[:])
+        rep = const.tile([P, P], F32, name="rep")
+        nc.vector.tensor_copy(out=rep[:], in_=muh_col[:].to_broadcast([P, P]))
+        pm = psum.tile([P, 512], F32, name="pm", tag="y0")
+        nc.tensor.transpose(pm[:, 0:P], rep[:], ident[:])
+        muh = const.tile([P, R], F32, name="muh")
+
+        for j in range(1, J):
+            tr_tile(0, j)
+            sq_tile(0, j)
+        for j in range(1, J):
+            exit_tile(0, j, False)
+        nc.vector.tensor_copy(out=muh[:], in_=pm[:, 0:P])
+
+        inv_sig_b = inv_sig[:].unsqueeze(1).to_broadcast([P, J, R])
+        phi2_b = phi2[:].unsqueeze(1).to_broadcast([P, J, R])
+
+        def mx(g):
+            codes, scales = q_tiles[g]
+            x_ps = psum.tile([P, 512], F32, name="x_ps", tag="x%d" % (g % 2))
+            y_ps = psum.tile([P, 512], F32, name="y_ps", tag="y%d" % (g % 2))
+            for j in range(J):
+                for c in range(2):
+                    zc = slice((j * 2 + c) * P, (j * 2 + c + 1) * P)
+                    for w, acc in ((0, x_ps), (1, y_ps)):
+                        wc = slice((c * 2 + w) * R, (c * 2 + w + 1) * R)
+                        nc.tensor.matmul_mx(
+                            out=acc[:, j * R : (j + 1) * R],
+                            lhsT=codes[:, zc].bitcast(FP8X4),
+                            lhsT_scale=scales[:, zc],
+                            rhs=w_codes[:, wc].bitcast(FP8X4),
+                            rhs_scale=w_scales[:, wc],
+                            start=(c == 0),
+                            stop=(c == 1),
+                        )
+            xy_tiles[g] = (x_ps, y_ps)
+
+        def window_arg(g):
+            x_ps = xy_tiles[g][0]
+            u = work.tile([P, GT], F32, name="u")
+            for j in range(J):
+                js = slice(j * R, (j + 1) * R)
+                nc.vector.scalar_tensor_tensor(
+                    out=u[:, js],
+                    in0=x_ps[:, js],
+                    scalar=zh[:, g * J + j : g * J + j + 1],
+                    in1=muh[:],
+                    op0=ALU.subtract,
+                    op1=ALU.subtract,
+                )
+            v = vpool.tile([P, GT], F32, name="v")
+            nc.vector.scalar_tensor_tensor(
+                out=v[:].rearrange("p (j r) -> p j r", j=J),
+                in0=u[:].rearrange("p (j r) -> p j r", j=J),
+                scalar=0.0,
+                in1=inv_sig_b,
+                op0=ALU.min,
+                op1=ALU.mult,
+            )
+            v_tiles[g] = v
+
+        def phase_arg(g):
+            y_ps = xy_tiles[g][1]
+            wv = work.tile([P, GT], F32, name="wv")
+            nc.vector.scalar_tensor_tensor(
+                out=wv[:].rearrange("p (j r) -> p j r", j=J),
+                in0=y_ps[:].rearrange("p (j r) -> p j r", j=J),
+                scalar=INV_TWO_PI,
+                in1=phi2_b,
+                op0=ALU.mult,
+                op1=ALU.add,
+            )
+            n_i = work.tile([P, GT], I32, name="n_i")
+            nc.vector.tensor_copy(out=n_i[:], in_=wv[:])
+            nc.vector.tensor_tensor(out=f_all[:, g * GT : (g + 1) * GT], in0=wv[:], in1=n_i[:], op=ALU.subtract)
+
+        def ex(g):
+            v = v_tiles[g]
+            for j in range(J):
+                nc.scalar.activation(
+                    out=e_all[:, g * GT + j * R : g * GT + (j + 1) * R],
+                    in_=v[:, j * R : (j + 1) * R],
+                    func=ACT.Exp,
+                    accum_out=ssum[:, g * J + j : g * J + j + 1],
+                )
+
+        def sin_groups(g0, g1):
+            nc.scalar.activation(
+                out=f_all[:, g0 * GT : g1 * GT], in_=f_all[:, g0 * GT : g1 * GT], func=ACT.Sin, scale=TWO_PI
+            )
+
+        def recip_sums(g0, g1):
+            gs = slice(g0 * J, g1 * J)
+            nc.vector.tensor_scalar_max(out=rs[:, gs], in0=ssum[:, gs], scalar1=1e-6)
+            nc.vector.reciprocal(out=rs[:, gs], in_=rs[:, gs])
+
+        def fin(g):
+            for j in range(J):
+                cs = slice(g * GT + j * R, g * GT + (j + 1) * R)
+                nc.vector.scalar_tensor_tensor(
+                    out=e_all[:, cs],
+                    in0=e_all[:, cs],
+                    scalar=rs[:, g * J + j : g * J + j + 1],
+                    in1=f_all[:, cs],
+                    op0=ALU.mult,
+                    op1=ALU.mult,
+                )
+            nc.sync.dma_start(out=o_groups[g], in_=e_all[:, g * GT : (g + 1) * GT])
+
+        for i in range(NG):
+            nxt = i + 1
+            if i >= 1:
+                mx(i - 1)
+            if i >= 1:
+                for j in range(J):
+                    if not (j == 0 and i in S_EXIT_GROUPS):
+                        exit_tile(i, j, False)
+            if nxt < NG:
+                new_grp(nxt)
+                for j in range(J):
+                    tr_tile(nxt, j)
+                    if j == 0 and nxt in S_EXIT_GROUPS:
+                        exit_tile(nxt, 0, True)
+            if i >= 3:
+                ex(i - 3)
+            if nxt < NG:
+                sq(nxt)
+            if nxt + NZ - 1 < NG:
+                load(nxt + NZ - 1)
+            if i >= 2:
+                window_arg(i - 2)
+                phase_arg(i - 2)
+            quant(i)
+        mx(NG - 1)
+        ex(NG - 3)
+        window_arg(NG - 2)
+        phase_arg(NG - 2)
+        ex(NG - 2)
+        window_arg(NG - 1)
+        ex(NG - 1)
+        phase_arg(NG - 1)
+        recip_sums(0, NG - 1)
+        sin_groups(0, 1)
+        sin_groups(1, 2)
+        for g0 in range(2, NG, 2):
+            sin_groups(g0, g0 + 2)
+        recip_sums(NG - 1, NG)
+        for g in range(NG):
+            fin(g)

@@ -22,7 +22,9 @@ GT = P * J
 NG = TOKENS // GT
 NZ = 5
 NXT = 4
-S_EXIT_GROUPS = (2, 4, 6, 8, 10, 12, 14, 15)
+S_EXIT_GROUPS = (1, 2, 4, 6, 8, 10, 12, 14, 15)
+LATE_FROM = 12
+SIN_CHUNKS = ((0, 1), (1, 2), (2, 4), (4, 6), (6, 8), (8, 10), (10, 12), (12, 14), (14, 15), (15, 16))
 
 FLOPS = 2 * 2 * TOKENS * R * D
 
@@ -134,7 +136,6 @@ def tile_gaborbasis_t_kernel(tc, z, mu, K, log_sigma, phi, out):
         new_grp(0)
         tr_tile(0, 0)
         sq_tile(0, 0)
-        exit_tile(0, 0, False)
 
         pb = psum.tile([P, 512], F32, name="pb", tag="x0")
         nc.tensor.matmul(pb[:, 0 : 2 * R], lhsT=ones_bf[:], rhs=rows[:], start=True, stop=True)
@@ -179,8 +180,6 @@ def tile_gaborbasis_t_kernel(tc, z, mu, K, log_sigma, phi, out):
         for j in range(1, J):
             tr_tile(0, j)
             sq_tile(0, j)
-        for j in range(1, J):
-            exit_tile(0, j, False)
         nc.vector.tensor_copy(out=muh[:], in_=pm[:, 0:P])
 
         inv_sig_b = inv_sig[:].unsqueeze(1).to_broadcast([P, J, R])
@@ -206,7 +205,11 @@ def tile_gaborbasis_t_kernel(tc, z, mu, K, log_sigma, phi, out):
                         )
             xy_tiles[g] = (x_ps, y_ps)
 
-        def window_arg(g):
+        u_tiles = {}
+        wv_tiles = {}
+        n_tiles = {}
+
+        def p1(g):
             x_ps = xy_tiles[g][0]
             u = work.tile([P, GT], F32, name="u")
             for j in range(J):
@@ -219,10 +222,13 @@ def tile_gaborbasis_t_kernel(tc, z, mu, K, log_sigma, phi, out):
                     op0=ALU.subtract,
                     op1=ALU.subtract,
                 )
+            u_tiles[g] = u
+
+        def p2(g):
             v = vpool.tile([P, GT], F32, name="v")
             nc.vector.scalar_tensor_tensor(
                 out=v[:].rearrange("p (j r) -> p j r", j=J),
-                in0=u[:].rearrange("p (j r) -> p j r", j=J),
+                in0=u_tiles[g][:].rearrange("p (j r) -> p j r", j=J),
                 scalar=0.0,
                 in1=inv_sig_b,
                 op0=ALU.min,
@@ -230,9 +236,9 @@ def tile_gaborbasis_t_kernel(tc, z, mu, K, log_sigma, phi, out):
             )
             v_tiles[g] = v
 
-        def phase_arg(g):
+        def p4(g):
             y_ps = xy_tiles[g][1]
-            wv = work.tile([P, GT], F32, name="wv")
+            wv = work.tile([P, GT], F32, name="wv", bufs=NG - LATE_FROM + 1)
             nc.vector.scalar_tensor_tensor(
                 out=wv[:].rearrange("p (j r) -> p j r", j=J),
                 in0=y_ps[:].rearrange("p (j r) -> p j r", j=J),
@@ -241,9 +247,17 @@ def tile_gaborbasis_t_kernel(tc, z, mu, K, log_sigma, phi, out):
                 op0=ALU.mult,
                 op1=ALU.add,
             )
+            wv_tiles[g] = wv
+
+        def p5(g):
             n_i = work.tile([P, GT], I32, name="n_i")
-            nc.vector.tensor_copy(out=n_i[:], in_=wv[:])
-            nc.vector.tensor_tensor(out=f_all[:, g * GT : (g + 1) * GT], in0=wv[:], in1=n_i[:], op=ALU.subtract)
+            nc.vector.tensor_copy(out=n_i[:], in_=wv_tiles[g][:])
+            n_tiles[g] = n_i
+
+        def p6(g):
+            nc.vector.tensor_tensor(
+                out=f_all[:, g * GT : (g + 1) * GT], in0=wv_tiles[g][:], in1=n_tiles[g][:], op=ALU.subtract
+            )
 
         def ex(g):
             v = v_tiles[g]
@@ -260,11 +274,6 @@ def tile_gaborbasis_t_kernel(tc, z, mu, K, log_sigma, phi, out):
                 out=f_all[:, g0 * GT : g1 * GT], in_=f_all[:, g0 * GT : g1 * GT], func=ACT.Sin, scale=TWO_PI
             )
 
-        def recip_sums(g0, g1):
-            gs = slice(g0 * J, g1 * J)
-            nc.vector.tensor_scalar_max(out=rs[:, gs], in0=ssum[:, gs], scalar1=1e-6)
-            nc.vector.reciprocal(out=rs[:, gs], in_=rs[:, gs])
-
         def fin(g):
             for j in range(J):
                 cs = slice(g * GT + j * R, g * GT + (j + 1) * R)
@@ -278,43 +287,61 @@ def tile_gaborbasis_t_kernel(tc, z, mu, K, log_sigma, phi, out):
                 )
             nc.sync.dma_start(out=o_groups[g], in_=e_all[:, g * GT : (g + 1) * GT])
 
-        for i in range(NG):
-            nxt = i + 1
-            if i >= 1:
+        def on_scalar(g, j):
+            return j == 0 and g in S_EXIT_GROUPS
+
+        def turn(g, j):
+            if not on_scalar(g, j):
+                exit_tile(g, j, False)
+            if g + 1 < NG:
+                tr_tile(g + 1, j)
+                if on_scalar(g + 1, j):
+                    exit_tile(g + 1, j, True)
+
+        for i in range(NG + 2):
+            a = i - 2
+            late = a >= LATE_FROM
+            if 0 <= a:
+                p1(a)
+            if 1 <= i <= NG:
+                quant(i - 1)
                 mx(i - 1)
-            if i >= 1:
-                for j in range(J):
-                    if not (j == 0 and i in S_EXIT_GROUPS):
-                        exit_tile(i, j, False)
-            if nxt < NG:
-                new_grp(nxt)
-                for j in range(J):
-                    tr_tile(nxt, j)
-                    if j == 0 and nxt in S_EXIT_GROUPS:
-                        exit_tile(nxt, 0, True)
+            if i + 1 < NG:
+                new_grp(i + 1)
             if i >= 3:
                 ex(i - 3)
-            if nxt < NG:
-                sq(nxt)
-            if nxt + NZ - 1 < NG:
-                load(nxt + NZ - 1)
-            if i >= 2:
-                window_arg(i - 2)
-                phase_arg(i - 2)
-            quant(i)
-        mx(NG - 1)
-        ex(NG - 3)
-        window_arg(NG - 2)
-        phase_arg(NG - 2)
-        ex(NG - 2)
-        window_arg(NG - 1)
+            if 0 <= a:
+                if i >= NG:
+                    p2(a)
+                    p4(a)
+                else:
+                    p4(a)
+                    p2(a)
+            if i < NG:
+                turn(i, 0)
+                turn(i, 1)
+            if 0 <= a and not late:
+                p5(a)
+            if i < NG:
+                turn(i, 2)
+            if 0 <= a and not late:
+                p6(a)
+            if i < NG:
+                turn(i, 3)
+            if i + 1 < NG:
+                sq(i + 1)
+            if i + NZ < NG:
+                load(i + NZ)
         ex(NG - 1)
-        phase_arg(NG - 1)
-        recip_sums(0, NG - 1)
-        sin_groups(0, 1)
-        sin_groups(1, 2)
-        for g0 in range(2, NG, 2):
-            sin_groups(g0, g0 + 2)
-        recip_sums(NG - 1, NG)
+        p5(LATE_FROM)
+        for g in range(LATE_FROM, NG):
+            if g + 1 < NG:
+                p5(g + 1)
+            else:
+                nc.vector.tensor_scalar_max(out=rs[:], in0=ssum[:], scalar1=1e-6)
+            p6(g)
+        nc.vector.reciprocal(out=rs[:], in_=rs[:])
+        for g0, g1 in SIN_CHUNKS:
+            sin_groups(g0, g1)
         for g in range(NG):
             fin(g)

@@ -22,7 +22,8 @@ GT = P * J
 NG = TOKENS // GT
 NZ = 5
 NXT = 4
-S_EXIT_GROUPS = (1, 2, 4, 6, 8, 10, 12, 14, 15)
+S_EXIT_GROUPS = (1, 2, 3, 4, 6, 8, 10, 12, 14, 15,)
+SX_POS = 0
 LATE_FROM = 12
 SIN_CHUNKS = ((0, 1), (1, 2), (2, 4), (4, 6), (6, 8), (8, 10), (10, 12), (12, 14), (14, 15), (15, 16))
 
@@ -68,13 +69,14 @@ def tile_gaborbasis_t_kernel(tc, z, mu, K, log_sigma, phi, out):
         nc.vector.memset(rows[:], 0.0)
         wk = const.tile([P, 2 * D], BF16, name="wk")
         new_z(0)
-        load_part(0, 0)
         nc.sync.dma_start(out=rows[0:1, 0:R], in_=log_sigma.unsqueeze(0))
         nc.sync.dma_start(out=rows[0:1, R : 2 * R], in_=phi.unsqueeze(0))
+        load_part(0, 0)
+        load_part(0, 1)
         nc.sync.dma_start(out=wk[:, 0:D], in_=mu)
         nc.sync.dma_start(out=wk[:, D : 2 * D], in_=K)
-        for j in range(1, J):
-            load_part(0, j)
+        load_part(0, 2)
+        load_part(0, 3)
         for g in range(1, NZ):
             load(g)
 
@@ -134,25 +136,36 @@ def tile_gaborbasis_t_kernel(tc, z, mu, K, log_sigma, phi, out):
             q_tiles[g] = (codes, scales)
 
         new_grp(0)
-        tr_tile(0, 0)
-        sq_tile(0, 0)
-
         pb = psum.tile([P, 512], F32, name="pb", tag="x0")
         nc.tensor.matmul(pb[:, 0 : 2 * R], lhsT=ones_bf[:], rhs=rows[:], start=True, stop=True)
         bc = const.tile([P, 2 * R], F32, name="bc")
         nc.vector.tensor_copy(out=bc[:], in_=pb[:, 0 : 2 * R])
+        tr_tile(0, 0)
+        sq_tile(0, 0)
+        exit_tile(0, 0, False)
         inv_sig = const.tile([P, R], F32, name="inv_sig")
         nc.scalar.activation(out=inv_sig[:], in_=bc[:, 0:R], func=ACT.Exp, scale=2.0)
         phi2 = const.tile([P, R], F32, name="phi2")
         nc.vector.tensor_scalar(
             out=phi2[:], in0=bc[:, R : 2 * R], scalar1=HALF_PI, scalar2=INV_TWO_PI, op0=ALU.add, op1=ALU.mult
         )
+        tr_tile(0, 1)
+        sq_tile(0, 1)
+        exit_tile(0, 1, False)
+        nc.vector.tensor_scalar_add(out=inv_sig[:], in0=inv_sig[:], scalar1=1e-8)
 
         wk_w = wk[:].bitcast(F32)
         gwk = const.tile([P, 2 * 2 * R * 4], BF16, name="gwk", align_bytes=64)
         gwk_w = gwk[:].bitcast(F32).rearrange("p (c w r u) -> p c w r u", c=2, w=2, u=2)
+        w_codes = const.tile([P, 4 * R], U32, name="w_codes", align_bytes=64)
+        w_scales = const.tile([P, 4 * R], U8, name="w_scales", align_bytes=64)
+        junk0 = work.tile([P, D], BF16, name="junk")
+        muh_col = const.tile([P, 1], F32, name="muh_col")
+        nc.scalar.activation(
+            out=junk0[:], in_=wk[:, 0:D], func=ACT.Square, scale=SQRT_HALF, accum_out=muh_col[:]
+        )
         for w in range(2):
-            wt = psum.tile([P, 512], F32, name="wt", tag="xt%d" % (2 + w))
+            wt = psum.tile([P, 512], F32, name="wt", tag="xy"[w] + "1")
             for cu in range(4):
                 nc.tensor.transpose(
                     wt[:, cu * P : (cu + 1) * P], wk_w[:, w * 512 + cu * P : w * 512 + (cu + 1) * P], ident[:]
@@ -160,27 +173,21 @@ def tile_gaborbasis_t_kernel(tc, z, mu, K, log_sigma, phi, out):
             nc.vector.tensor_copy(
                 out=gwk_w[:, :, w, :, :], in_=wt[:].rearrange("p (c u r) -> p c r u", c=2, u=2)
             )
-        w_codes = const.tile([P, 4 * R], U32, name="w_codes", align_bytes=64)
-        w_scales = const.tile([P, 4 * R], U8, name="w_scales", align_bytes=64)
-
-        junk0 = work.tile([P, D], BF16, name="junk")
-        muh_col = const.tile([P, 1], F32, name="muh_col")
-        nc.scalar.activation(
-            out=junk0[:], in_=wk[:, 0:D], func=ACT.Square, scale=SQRT_HALF, accum_out=muh_col[:]
-        )
-        nc.vector.tensor_scalar_add(out=inv_sig[:], in0=inv_sig[:], scalar1=1e-8)
-        nc.vector.reciprocal(out=inv_sig[:], in_=inv_sig[:])
-        nc.vector.quantize_mx(out=w_codes[:].bitcast(FP8X4), scales=w_scales[:], in_=gwk[:])
+            if w == 0:
+                nc.vector.reciprocal(out=inv_sig[:], in_=inv_sig[:])
         rep = const.tile([P, P], F32, name="rep")
         nc.vector.tensor_copy(out=rep[:], in_=muh_col[:].to_broadcast([P, P]))
         pm = psum.tile([P, 512], F32, name="pm", tag="y0")
         nc.tensor.transpose(pm[:, 0:P], rep[:], ident[:])
+        tr_tile(0, 2)
+        sq_tile(0, 2)
+        tr_tile(0, 3)
+        sq_tile(0, 3)
+        exit_tile(0, 2, False)
         muh = const.tile([P, R], F32, name="muh")
-
-        for j in range(1, J):
-            tr_tile(0, j)
-            sq_tile(0, j)
         nc.vector.tensor_copy(out=muh[:], in_=pm[:, 0:P])
+        exit_tile(0, 3, False)
+        nc.vector.quantize_mx(out=w_codes[:].bitcast(FP8X4), scales=w_scales[:], in_=gwk[:])
 
         inv_sig_b = inv_sig[:].unsqueeze(1).to_broadcast([P, J, R])
         phi2_b = phi2[:].unsqueeze(1).to_broadcast([P, J, R])
@@ -250,7 +257,7 @@ def tile_gaborbasis_t_kernel(tc, z, mu, K, log_sigma, phi, out):
             wv_tiles[g] = wv
 
         def p5(g):
-            n_i = work.tile([P, GT], I32, name="n_i")
+            n_i = work.tile([P, GT], I32, name="n_i", bufs=max(2, NG - 2 - LATE_FROM))
             nc.vector.tensor_copy(out=n_i[:], in_=wv_tiles[g][:])
             n_tiles[g] = n_i
 
@@ -291,55 +298,61 @@ def tile_gaborbasis_t_kernel(tc, z, mu, K, log_sigma, phi, out):
             return j == 0 and g in S_EXIT_GROUPS
 
         def turn(g, j):
-            if not on_scalar(g, j):
+            if g > 0 and not on_scalar(g, j):
                 exit_tile(g, j, False)
             if g + 1 < NG:
                 tr_tile(g + 1, j)
-                if on_scalar(g + 1, j):
-                    exit_tile(g + 1, j, True)
 
-        for i in range(NG + 2):
+        for i in range(NG):
             a = i - 2
             late = a >= LATE_FROM
-            if 0 <= a:
-                p1(a)
-            if 1 <= i <= NG:
+            if i >= 1:
                 quant(i - 1)
                 mx(i - 1)
+            if 0 <= a:
+                p1(a)
             if i + 1 < NG:
                 new_grp(i + 1)
             if i >= 3:
                 ex(i - 3)
             if 0 <= a:
-                if i >= NG:
-                    p2(a)
-                    p4(a)
-                else:
-                    p4(a)
-                    p2(a)
-            if i < NG:
-                turn(i, 0)
-                turn(i, 1)
+                p4(a)
+                p2(a)
+            turn(i, 0)
+            turn(i, 1)
             if 0 <= a and not late:
                 p5(a)
-            if i < NG:
-                turn(i, 2)
+            turn(i, 2)
+            turn(i, 3)
             if 0 <= a and not late:
                 p6(a)
-            if i < NG:
-                turn(i, 3)
             if i + 1 < NG:
-                sq(i + 1)
+                for j in range(J):
+                    if j == SX_POS and on_scalar(i + 1, 0):
+                        exit_tile(i + 1, 0, True)
+                    sq_tile(i + 1, j)
             if i + NZ < NG:
                 load(i + NZ)
-        ex(NG - 1)
-        p5(LATE_FROM)
-        for g in range(LATE_FROM, NG):
-            if g + 1 < NG:
-                p5(g + 1)
-            else:
-                nc.vector.tensor_scalar_max(out=rs[:], in0=ssum[:], scalar1=1e-6)
+        p1(NG - 2)
+        quant(NG - 1)
+        mx(NG - 1)
+        ex(NG - 3)
+        p2(NG - 2)
+        ex(NG - 2)
+        p4(NG - 2)
+        for g in range(LATE_FROM, NG - 2):
+            p5(g)
+        for g in range(LATE_FROM, NG - 2):
             p6(g)
+        p1(NG - 1)
+        p5(NG - 2)
+        p2(NG - 1)
+        ex(NG - 1)
+        p4(NG - 1)
+        p6(NG - 2)
+        p5(NG - 1)
+        nc.vector.tensor_scalar_max(out=rs[:], in0=ssum[:], scalar1=1e-6)
+        p6(NG - 1)
         nc.vector.reciprocal(out=rs[:], in_=rs[:])
         for g0, g1 in SIN_CHUNKS:
             sin_groups(g0, g1)

@@ -20,10 +20,13 @@ TOKENS = 8192
 J = 4
 GT = P * J
 NG = TOKENS // GT
+PASSES = 2
+BANK = 512
+WORDS = D // 2
 NZ = 5
 NXT = 4
-S_EXIT_GROUPS = (1, 2, 3, 4, 6, 8, 10, 12, 14, 15,)
-SX_POS = 0
+
+SCALAR_COPY_GROUPS = (1, 2, 3, 4, 5, 6, 7, 8, 9, 10, 11, 12, 13, 14, 15)
 LATE_FROM = 12
 SIN_CHUNKS = ((0, 1), (1, 2), (2, 4), (4, 6), (6, 8), (8, 10), (10, 12), (12, 14), (14, 15), (15, 16))
 
@@ -53,7 +56,10 @@ def tile_gaborbasis_t_kernel(tc, z, mu, K, log_sigma, phi, out):
         grp_tiles = {}
         q_tiles = {}
         xy_tiles = {}
+        u_tiles = {}
         v_tiles = {}
+        w_tiles = {}
+        n_tiles = {}
 
         def new_z(g):
             z_tiles[g] = zpool.tile([P, J * D], BF16, name="z_sb")
@@ -62,7 +68,7 @@ def tile_gaborbasis_t_kernel(tc, z, mu, K, log_sigma, phi, out):
             new_z(g)
             nc.sync.dma_start(out=z_tiles[g][:].rearrange("p (j k) -> p j k", j=J), in_=z_groups[g])
 
-        def load_part(g, j):
+        def load_tile(g, j):
             nc.sync.dma_start(out=z_tiles[g][:, j * D : (j + 1) * D], in_=z_groups[g][:, j, :])
 
         rows = const.tile([P, 2 * R], BF16, name="rows")
@@ -71,12 +77,12 @@ def tile_gaborbasis_t_kernel(tc, z, mu, K, log_sigma, phi, out):
         new_z(0)
         nc.sync.dma_start(out=rows[0:1, 0:R], in_=log_sigma.unsqueeze(0))
         nc.sync.dma_start(out=rows[0:1, R : 2 * R], in_=phi.unsqueeze(0))
-        load_part(0, 0)
-        load_part(0, 1)
+        load_tile(0, 0)
+        load_tile(0, 1)
         nc.sync.dma_start(out=wk[:, 0:D], in_=mu)
         nc.sync.dma_start(out=wk[:, D : 2 * D], in_=K)
-        load_part(0, 2)
-        load_part(0, 3)
+        load_tile(0, 2)
+        load_tile(0, 3)
         for g in range(1, NZ):
             load(g)
 
@@ -94,7 +100,7 @@ def tile_gaborbasis_t_kernel(tc, z, mu, K, log_sigma, phi, out):
         f_all = const.tile([P, TOKENS], F32, name="f_all")
         e_all = const.tile([P, TOKENS], F32, name="e_all")
 
-        def sq_tile(g, j):
+        def half_square_sum(g, j):
             junk = work.tile([P, D], BF16, name="junk")
             nc.scalar.activation(
                 out=junk[:],
@@ -104,101 +110,101 @@ def tile_gaborbasis_t_kernel(tc, z, mu, K, log_sigma, phi, out):
                 accum_out=zh[:, g * J + j : g * J + j + 1],
             )
 
-        def sq(g):
-            for j in range(J):
-                sq_tile(g, j)
-
-        def tr_tile(g, j):
+        def transpose_tile(g, j):
             z_w = z_tiles[g][:].bitcast(F32)
             t = g * J + j
-            xt = psum.tile([P, 512], F32, name="xt", tag="xt%d" % (t % NXT))
+            xt = psum.tile([P, BANK], F32, name="xt", tag="xt%d" % (t % NXT))
             for cu in range(4):
                 nc.tensor.transpose(
-                    xt[:, cu * P : (cu + 1) * P], z_w[:, j * 512 + cu * P : j * 512 + (cu + 1) * P], ident[:]
+                    xt[:, cu * P : (cu + 1) * P],
+                    z_w[:, j * WORDS + cu * P : j * WORDS + (cu + 1) * P],
+                    ident[:],
                 )
             xt_tiles[t] = xt
 
         def new_grp(g):
             grp_tiles[g] = work.tile([P, J * D], BF16, name="grp", align_bytes=64)
 
-        def exit_tile(g, j, on_scalar):
-            grp_w = grp_tiles[g][:].bitcast(F32).rearrange("p (j c t u) -> p j c t u", j=J, c=2, u=2)
-            src = xt_tiles[g * J + j][:].rearrange("p (c u t) -> p c t u", c=2, u=2)
+        def copy_out(g, j, on_scalar):
+            grp_w = grp_tiles[g][:].bitcast(F32).rearrange("p (j c t u) -> p j c t u", j=J, c=PASSES, u=2)
+            src = xt_tiles[g * J + j][:].rearrange("p (c u t) -> p c t u", c=PASSES, u=2)
             if on_scalar:
                 nc.scalar.copy(out=grp_w[:, j, :, :, :], in_=src)
             else:
                 nc.vector.tensor_copy(out=grp_w[:, j, :, :, :], in_=src)
 
-        def quant(g):
-            codes = work.tile([P, J * 2 * P], U32, name="codes", align_bytes=64)
-            scales = work.tile([P, J * 2 * P], U8, name="scales", align_bytes=64)
+        def quantise(g):
+            codes = work.tile([P, J * PASSES * P], U32, name="codes", align_bytes=64)
+            scales = work.tile([P, J * PASSES * P], U8, name="scales", align_bytes=64)
             nc.vector.quantize_mx(out=codes[:].bitcast(FP8X4), scales=scales[:], in_=grp_tiles[g][:])
             q_tiles[g] = (codes, scales)
 
         new_grp(0)
-        pb = psum.tile([P, 512], F32, name="pb", tag="x0")
+        pb = psum.tile([P, BANK], F32, name="pb", tag="x0")
         nc.tensor.matmul(pb[:, 0 : 2 * R], lhsT=ones_bf[:], rhs=rows[:], start=True, stop=True)
         bc = const.tile([P, 2 * R], F32, name="bc")
         nc.vector.tensor_copy(out=bc[:], in_=pb[:, 0 : 2 * R])
-        tr_tile(0, 0)
-        sq_tile(0, 0)
-        exit_tile(0, 0, False)
+        transpose_tile(0, 0)
+        half_square_sum(0, 0)
+        copy_out(0, 0, False)
         inv_sig = const.tile([P, R], F32, name="inv_sig")
         nc.scalar.activation(out=inv_sig[:], in_=bc[:, 0:R], func=ACT.Exp, scale=2.0)
         phi2 = const.tile([P, R], F32, name="phi2")
         nc.vector.tensor_scalar(
             out=phi2[:], in0=bc[:, R : 2 * R], scalar1=HALF_PI, scalar2=INV_TWO_PI, op0=ALU.add, op1=ALU.mult
         )
-        tr_tile(0, 1)
-        sq_tile(0, 1)
-        exit_tile(0, 1, False)
+        transpose_tile(0, 1)
+        half_square_sum(0, 1)
+        copy_out(0, 1, False)
         nc.vector.tensor_scalar_add(out=inv_sig[:], in0=inv_sig[:], scalar1=1e-8)
 
         wk_w = wk[:].bitcast(F32)
-        gwk = const.tile([P, 2 * 2 * R * 4], BF16, name="gwk", align_bytes=64)
-        gwk_w = gwk[:].bitcast(F32).rearrange("p (c w r u) -> p c w r u", c=2, w=2, u=2)
-        w_codes = const.tile([P, 4 * R], U32, name="w_codes", align_bytes=64)
-        w_scales = const.tile([P, 4 * R], U8, name="w_scales", align_bytes=64)
+        gwk = const.tile([P, PASSES * 2 * R * 4], BF16, name="gwk", align_bytes=64)
+        gwk_w = gwk[:].bitcast(F32).rearrange("p (c w r u) -> p c w r u", c=PASSES, w=2, u=2)
+        w_codes = const.tile([P, PASSES * 2 * R], U32, name="w_codes", align_bytes=64)
+        w_scales = const.tile([P, PASSES * 2 * R], U8, name="w_scales", align_bytes=64)
         junk0 = work.tile([P, D], BF16, name="junk")
         muh_col = const.tile([P, 1], F32, name="muh_col")
         nc.scalar.activation(
             out=junk0[:], in_=wk[:, 0:D], func=ACT.Square, scale=SQRT_HALF, accum_out=muh_col[:]
         )
         for w in range(2):
-            wt = psum.tile([P, 512], F32, name="wt", tag="xy"[w] + "1")
+            wt = psum.tile([P, BANK], F32, name="wt", tag="xy"[w] + "1")
             for cu in range(4):
                 nc.tensor.transpose(
-                    wt[:, cu * P : (cu + 1) * P], wk_w[:, w * 512 + cu * P : w * 512 + (cu + 1) * P], ident[:]
+                    wt[:, cu * P : (cu + 1) * P],
+                    wk_w[:, w * WORDS + cu * P : w * WORDS + (cu + 1) * P],
+                    ident[:],
                 )
             nc.vector.tensor_copy(
-                out=gwk_w[:, :, w, :, :], in_=wt[:].rearrange("p (c u r) -> p c r u", c=2, u=2)
+                out=gwk_w[:, :, w, :, :], in_=wt[:].rearrange("p (c u r) -> p c r u", c=PASSES, u=2)
             )
             if w == 0:
                 nc.vector.reciprocal(out=inv_sig[:], in_=inv_sig[:])
         rep = const.tile([P, P], F32, name="rep")
         nc.vector.tensor_copy(out=rep[:], in_=muh_col[:].to_broadcast([P, P]))
-        pm = psum.tile([P, 512], F32, name="pm", tag="y0")
+        pm = psum.tile([P, BANK], F32, name="pm", tag="y0")
         nc.tensor.transpose(pm[:, 0:P], rep[:], ident[:])
-        tr_tile(0, 2)
-        sq_tile(0, 2)
-        tr_tile(0, 3)
-        sq_tile(0, 3)
-        exit_tile(0, 2, False)
+        transpose_tile(0, 2)
+        half_square_sum(0, 2)
+        transpose_tile(0, 3)
+        half_square_sum(0, 3)
+        copy_out(0, 2, False)
         muh = const.tile([P, R], F32, name="muh")
         nc.vector.tensor_copy(out=muh[:], in_=pm[:, 0:P])
-        exit_tile(0, 3, False)
+        copy_out(0, 3, False)
         nc.vector.quantize_mx(out=w_codes[:].bitcast(FP8X4), scales=w_scales[:], in_=gwk[:])
 
         inv_sig_b = inv_sig[:].unsqueeze(1).to_broadcast([P, J, R])
         phi2_b = phi2[:].unsqueeze(1).to_broadcast([P, J, R])
 
-        def mx(g):
+        def mx_passes(g):
             codes, scales = q_tiles[g]
-            x_ps = psum.tile([P, 512], F32, name="x_ps", tag="x%d" % (g % 2))
-            y_ps = psum.tile([P, 512], F32, name="y_ps", tag="y%d" % (g % 2))
+            x_ps = psum.tile([P, BANK], F32, name="x_ps", tag="x%d" % (g % 2))
+            y_ps = psum.tile([P, BANK], F32, name="y_ps", tag="y%d" % (g % 2))
             for j in range(J):
-                for c in range(2):
-                    zc = slice((j * 2 + c) * P, (j * 2 + c + 1) * P)
+                for c in range(PASSES):
+                    zc = slice((j * PASSES + c) * P, (j * PASSES + c + 1) * P)
                     for w, acc in ((0, x_ps), (1, y_ps)):
                         wc = slice((c * 2 + w) * R, (c * 2 + w + 1) * R)
                         nc.tensor.matmul_mx(
@@ -208,15 +214,11 @@ def tile_gaborbasis_t_kernel(tc, z, mu, K, log_sigma, phi, out):
                             rhs=w_codes[:, wc].bitcast(FP8X4),
                             rhs_scale=w_scales[:, wc],
                             start=(c == 0),
-                            stop=(c == 1),
+                            stop=(c == PASSES - 1),
                         )
             xy_tiles[g] = (x_ps, y_ps)
 
-        u_tiles = {}
-        wv_tiles = {}
-        n_tiles = {}
-
-        def p1(g):
+        def neg_half_dsq(g):
             x_ps = xy_tiles[g][0]
             u = work.tile([P, GT], F32, name="u")
             for j in range(J):
@@ -231,7 +233,7 @@ def tile_gaborbasis_t_kernel(tc, z, mu, K, log_sigma, phi, out):
                 )
             u_tiles[g] = u
 
-        def p2(g):
+        def exp_argument(g):
             v = vpool.tile([P, GT], F32, name="v")
             nc.vector.scalar_tensor_tensor(
                 out=v[:].rearrange("p (j r) -> p j r", j=J),
@@ -243,30 +245,30 @@ def tile_gaborbasis_t_kernel(tc, z, mu, K, log_sigma, phi, out):
             )
             v_tiles[g] = v
 
-        def p4(g):
+        def phase_turns(g):
             y_ps = xy_tiles[g][1]
-            wv = work.tile([P, GT], F32, name="wv", bufs=NG - LATE_FROM + 1)
+            w_sb = work.tile([P, GT], F32, name="wv", bufs=NG - LATE_FROM + 1)
             nc.vector.scalar_tensor_tensor(
-                out=wv[:].rearrange("p (j r) -> p j r", j=J),
+                out=w_sb[:].rearrange("p (j r) -> p j r", j=J),
                 in0=y_ps[:].rearrange("p (j r) -> p j r", j=J),
                 scalar=INV_TWO_PI,
                 in1=phi2_b,
                 op0=ALU.mult,
                 op1=ALU.add,
             )
-            wv_tiles[g] = wv
+            w_tiles[g] = w_sb
 
-        def p5(g):
+        def round_turns(g):
             n_i = work.tile([P, GT], I32, name="n_i", bufs=max(2, NG - 2 - LATE_FROM))
-            nc.vector.tensor_copy(out=n_i[:], in_=wv_tiles[g][:])
+            nc.vector.tensor_copy(out=n_i[:], in_=w_tiles[g][:])
             n_tiles[g] = n_i
 
-        def p6(g):
+        def reduce_turns(g):
             nc.vector.tensor_tensor(
-                out=f_all[:, g * GT : (g + 1) * GT], in0=wv_tiles[g][:], in1=n_tiles[g][:], op=ALU.subtract
+                out=f_all[:, g * GT : (g + 1) * GT], in0=w_tiles[g][:], in1=n_tiles[g][:], op=ALU.subtract
             )
 
-        def ex(g):
+        def windows(g):
             v = v_tiles[g]
             for j in range(J):
                 nc.scalar.activation(
@@ -276,12 +278,12 @@ def tile_gaborbasis_t_kernel(tc, z, mu, K, log_sigma, phi, out):
                     accum_out=ssum[:, g * J + j : g * J + j + 1],
                 )
 
-        def sin_groups(g0, g1):
+        def sines(g0, g1):
             nc.scalar.activation(
                 out=f_all[:, g0 * GT : g1 * GT], in_=f_all[:, g0 * GT : g1 * GT], func=ACT.Sin, scale=TWO_PI
             )
 
-        def fin(g):
+        def product_and_store(g):
             for j in range(J):
                 cs = slice(g * GT + j * R, g * GT + (j + 1) * R)
                 nc.vector.scalar_tensor_tensor(
@@ -294,67 +296,69 @@ def tile_gaborbasis_t_kernel(tc, z, mu, K, log_sigma, phi, out):
                 )
             nc.sync.dma_start(out=o_groups[g], in_=e_all[:, g * GT : (g + 1) * GT])
 
-        def on_scalar(g, j):
-            return j == 0 and g in S_EXIT_GROUPS
+        def scalar_copies(g, j):
+            return j == 0 and g in SCALAR_COPY_GROUPS
 
-        def turn(g, j):
-            if g > 0 and not on_scalar(g, j):
-                exit_tile(g, j, False)
+        def turn_bank(g, j):
+            if g > 0 and not scalar_copies(g, j):
+                copy_out(g, j, False)
             if g + 1 < NG:
-                tr_tile(g + 1, j)
+                transpose_tile(g + 1, j)
 
         for i in range(NG):
             a = i - 2
             late = a >= LATE_FROM
             if i >= 1:
-                quant(i - 1)
-                mx(i - 1)
+                quantise(i - 1)
+                mx_passes(i - 1)
             if 0 <= a:
-                p1(a)
+                neg_half_dsq(a)
             if i + 1 < NG:
                 new_grp(i + 1)
             if i >= 3:
-                ex(i - 3)
+                windows(i - 3)
             if 0 <= a:
-                p4(a)
-                p2(a)
-            turn(i, 0)
-            turn(i, 1)
+                phase_turns(a)
+                exp_argument(a)
+            turn_bank(i, 0)
+            turn_bank(i, 1)
             if 0 <= a and not late:
-                p5(a)
-            turn(i, 2)
-            turn(i, 3)
+                round_turns(a)
+            turn_bank(i, 2)
+            turn_bank(i, 3)
             if 0 <= a and not late:
-                p6(a)
+                reduce_turns(a)
             if i + 1 < NG:
+                if scalar_copies(i + 1, 0):
+                    copy_out(i + 1, 0, True)
                 for j in range(J):
-                    if j == SX_POS and on_scalar(i + 1, 0):
-                        exit_tile(i + 1, 0, True)
-                    sq_tile(i + 1, j)
+                    half_square_sum(i + 1, j)
             if i + NZ < NG:
                 load(i + NZ)
-        p1(NG - 2)
-        quant(NG - 1)
-        mx(NG - 1)
-        ex(NG - 3)
-        p2(NG - 2)
-        ex(NG - 2)
-        p4(NG - 2)
+
+        neg_half_dsq(NG - 2)
+        quantise(NG - 1)
+        mx_passes(NG - 1)
+        windows(NG - 3)
+        exp_argument(NG - 2)
+        windows(NG - 2)
+        phase_turns(NG - 2)
         for g in range(LATE_FROM, NG - 2):
-            p5(g)
+            round_turns(g)
         for g in range(LATE_FROM, NG - 2):
-            p6(g)
-        p1(NG - 1)
-        p5(NG - 2)
-        p2(NG - 1)
-        ex(NG - 1)
-        p4(NG - 1)
-        p6(NG - 2)
-        p5(NG - 1)
+            reduce_turns(g)
+        neg_half_dsq(NG - 1)
+        round_turns(NG - 2)
+        exp_argument(NG - 1)
+        windows(NG - 1)
+        phase_turns(NG - 1)
+        reduce_turns(NG - 2)
+        round_turns(NG - 1)
         nc.vector.tensor_scalar_max(out=rs[:], in0=ssum[:], scalar1=1e-6)
-        p6(NG - 1)
+        reduce_turns(NG - 1)
         nc.vector.reciprocal(out=rs[:], in_=rs[:])
+
         for g0, g1 in SIN_CHUNKS:
-            sin_groups(g0, g1)
+            sines(g0, g1)
         for g in range(NG):
-            fin(g)
+            product_and_store(g)

@@ -26,7 +26,7 @@ WORDS = D // 2
 NZ = 5
 NXT = 4
 
-SCALAR_COPY_GROUPS = (1, 2, 3, 4, 5, 6, 7, 8, 9, 10, 11, 12, 13, 14, 15)
+SCALAR_COPY_GROUPS = (1, 2, 3, 4, 6, 8, 10, 12, 14, 15)
 LATE_FROM = 12
 SIN_CHUNKS = ((0, 1), (1, 2), (2, 4), (4, 6), (6, 8), (8, 10), (10, 12), (12, 14), (14, 15), (15, 16))
 
@@ -259,8 +259,8 @@ def tile_gaborbasis_t_kernel(tc, z, mu, K, log_sigma, phi, out):
             w_tiles[g] = w_sb
 
         def round_turns(g):
-            n_i = work.tile([P, GT], I32, name="n_i", bufs=max(2, NG - 2 - LATE_FROM))
-            nc.vector.tensor_copy(out=n_i[:], in_=w_tiles[g][:])
+            n_i = work.tile([P, GT], I32, name="n_i", bufs=NG - LATE_FROM + 1)
+            nc.gpsimd.tensor_scalar(out=n_i[:], in0=w_tiles[g][:], scalar1=1.0, scalar2=0.0, op0=ALU.mult, op1=ALU.add)
             n_tiles[g] = n_i
 
         def reduce_turns(g):
@@ -312,22 +312,19 @@ def tile_gaborbasis_t_kernel(tc, z, mu, K, log_sigma, phi, out):
                 quantise(i - 1)
                 mx_passes(i - 1)
             if 0 <= a:
+                phase_turns(a)
+                round_turns(a)
                 neg_half_dsq(a)
             if i + 1 < NG:
                 new_grp(i + 1)
             if i >= 3:
                 windows(i - 3)
+            for j in range(J):
+                turn_bank(i, j)
             if 0 <= a:
-                phase_turns(a)
                 exp_argument(a)
-            turn_bank(i, 0)
-            turn_bank(i, 1)
-            if 0 <= a and not late:
-                round_turns(a)
-            turn_bank(i, 2)
-            turn_bank(i, 3)
-            if 0 <= a and not late:
-                reduce_turns(a)
+                if not late:
+                    reduce_turns(a)
             if i + 1 < NG:
                 if scalar_copies(i + 1, 0):
                     copy_out(i + 1, 0, True)
@@ -336,29 +333,30 @@ def tile_gaborbasis_t_kernel(tc, z, mu, K, log_sigma, phi, out):
             if i + NZ < NG:
                 load(i + NZ)
 
-        neg_half_dsq(NG - 2)
         quantise(NG - 1)
         mx_passes(NG - 1)
         windows(NG - 3)
+        phase_turns(NG - 2)
+        round_turns(NG - 2)
+        neg_half_dsq(NG - 2)
+        reduce_turns(LATE_FROM)
         exp_argument(NG - 2)
         windows(NG - 2)
-        phase_turns(NG - 2)
-        for g in range(LATE_FROM, NG - 2):
-            round_turns(g)
-        for g in range(LATE_FROM, NG - 2):
+        for g in range(LATE_FROM + 1, NG - 2):
             reduce_turns(g)
         neg_half_dsq(NG - 1)
-        round_turns(NG - 2)
+        reduce_turns(NG - 2)
         exp_argument(NG - 1)
         windows(NG - 1)
         phase_turns(NG - 1)
-        reduce_turns(NG - 2)
         round_turns(NG - 1)
         nc.vector.tensor_scalar_max(out=rs[:], in0=ssum[:], scalar1=1e-6)
-        reduce_turns(NG - 1)
-        nc.vector.reciprocal(out=rs[:], in_=rs[:])
-
-        for g0, g1 in SIN_CHUNKS:
+        for g0, g1 in SIN_CHUNKS[:-1]:
             sines(g0, g1)
-        for g in range(NG):
+        nc.vector.reciprocal(out=rs[:], in_=rs[:])
+        product_and_store(0)
+        reduce_turns(NG - 1)
+        for g0, g1 in SIN_CHUNKS[-1:]:
+            sines(g0, g1)
+        for g in range(1, NG):
             product_and_store(g)

@@ -26,8 +26,10 @@ WORDS = D // 2
 NZ = 5
 NXT = 4
 
-SCALAR_COPY_GROUPS = (1, 2, 3, 4, 6, 8, 10, 12, 14, 15)
+SCALAR_COPY_GROUPS = (2, 4, 6, 8, 10, 12)
 LATE_FROM = 12
+POOL_ARG_GROUPS = (0, 2, 4, 6, 8, 10)
+LOWEST = -3.0e38
 SIN_CHUNKS = ((0, 1), (1, 2), (2, 4), (4, 6), (6, 8), (8, 10), (10, 12), (12, 14), (14, 15), (15, 16))
 
 FLOPS = 2 * 2 * TOKENS * R * D
@@ -48,7 +50,7 @@ def tile_gaborbasis_t_kernel(tc, z, mu, K, log_sigma, phi, out):
         const = ctx.enter_context(tc.tile_pool(name="const", bufs=1))
         zpool = ctx.enter_context(tc.tile_pool(name="zpool", bufs=NZ))
         work = ctx.enter_context(tc.tile_pool(name="work", bufs=2))
-        vpool = ctx.enter_context(tc.tile_pool(name="vpool", bufs=3))
+        vpool = ctx.enter_context(tc.tile_pool(name="vpool", bufs=4))
         psum = ctx.enter_context(tc.psum_pool(name="psum", bufs=1))
 
         z_tiles = {}
@@ -245,6 +247,21 @@ def tile_gaborbasis_t_kernel(tc, z, mu, K, log_sigma, phi, out):
             )
             v_tiles[g] = v
 
+        def pool_clamp(g):
+            nc.gpsimd.tensor_scalar(
+                out=u_tiles[g][:], in0=u_tiles[g][:], scalar1=0.0, scalar2=LOWEST, op0=ALU.min, op1=ALU.max
+            )
+
+        def pool_scale(g):
+            v = vpool.tile([P, GT], F32, name="v")
+            nc.gpsimd.tensor_tensor(
+                out=v[:].rearrange("p (j r) -> p j r", j=J),
+                in0=u_tiles[g][:].rearrange("p (j r) -> p j r", j=J),
+                in1=inv_sig_b,
+                op=ALU.mult,
+            )
+            v_tiles[g] = v
+
         def phase_turns(g):
             y_ps = xy_tiles[g][1]
             w_sb = work.tile([P, GT], F32, name="wv", bufs=NG - LATE_FROM + 1)
@@ -315,14 +332,19 @@ def tile_gaborbasis_t_kernel(tc, z, mu, K, log_sigma, phi, out):
                 phase_turns(a)
                 round_turns(a)
                 neg_half_dsq(a)
+                if a in POOL_ARG_GROUPS:
+                    pool_clamp(a)
+                if a - 1 in POOL_ARG_GROUPS:
+                    pool_scale(a - 1)
             if i + 1 < NG:
                 new_grp(i + 1)
-            if i >= 3:
-                windows(i - 3)
+            if i >= 4:
+                windows(i - 4)
             for j in range(J):
                 turn_bank(i, j)
             if 0 <= a:
-                exp_argument(a)
+                if a not in POOL_ARG_GROUPS:
+                    exp_argument(a)
                 if not late:
                     reduce_turns(a)
             if i + 1 < NG:
@@ -335,6 +357,7 @@ def tile_gaborbasis_t_kernel(tc, z, mu, K, log_sigma, phi, out):
 
         quantise(NG - 1)
         mx_passes(NG - 1)
+        windows(NG - 4)
         windows(NG - 3)
         phase_turns(NG - 2)
         round_turns(NG - 2)

@@ -26,7 +26,8 @@ WORDS = D // 2
 NZ = 5
 NXT = 4
 
-SCALAR_COPY_GROUPS = (2, 4, 6, 8, 10, 12)
+SCALAR_COPY_GROUPS = tuple(range(1, NG))
+GRAM_GROUPS = tuple(range(1, 13))
 LATE_FROM = 12
 POOL_ARG_GROUPS = (0, 2, 4, 6, 8, 10)
 LOWEST = -3.0e38
@@ -62,6 +63,7 @@ def tile_gaborbasis_t_kernel(tc, z, mu, K, log_sigma, phi, out):
         v_tiles = {}
         w_tiles = {}
         n_tiles = {}
+        gram_tiles = {}
 
         def new_z(g):
             z_tiles[g] = zpool.tile([P, J * D], BF16, name="z_sb")
@@ -134,6 +136,32 @@ def tile_gaborbasis_t_kernel(tc, z, mu, K, log_sigma, phi, out):
                 nc.scalar.copy(out=grp_w[:, j, :, :, :], in_=src)
             else:
                 nc.vector.tensor_copy(out=grp_w[:, j, :, :, :], in_=src)
+
+        def gram(g):
+            gz = grp_tiles[g][:].rearrange("p (j c t w) -> p j c t w", j=J, c=PASSES, w=4)
+            acc = psum.tile([P, BANK], F32, name="xt", tag="xt%d" % (g * J % NXT))
+            for c in range(PASSES):
+                for w in range(4):
+                    nc.tensor.matmul(
+                        acc[:, 0:P],
+                        lhsT=gz[:, 0, c, :, w],
+                        rhs=gz[:, 0, c, :, w],
+                        start=(c == 0 and w == 0),
+                        stop=(c == PASSES - 1 and w == 3),
+                    )
+            gram_tiles[g] = acc
+
+        def gram_diagonal(g):
+            dj = work.tile([P, P], F32, name="dj")
+            nc.vector.scalar_tensor_tensor(
+                out=dj[:],
+                in0=gram_tiles[g][:, 0:P],
+                scalar=0.5,
+                in1=ident[:],
+                op0=ALU.mult,
+                op1=ALU.mult,
+                accum_out=zh[:, g * J : g * J + 1],
+            )
 
         def quantise(g):
             codes = work.tile([P, J * PASSES * P], U32, name="codes", align_bytes=64)
@@ -325,9 +353,13 @@ def tile_gaborbasis_t_kernel(tc, z, mu, K, log_sigma, phi, out):
         for i in range(NG):
             a = i - 2
             late = a >= LATE_FROM
+            if i in GRAM_GROUPS:
+                gram(i)
             if i >= 1:
                 quantise(i - 1)
                 mx_passes(i - 1)
+            if i in GRAM_GROUPS:
+                gram_diagonal(i)
             if 0 <= a:
                 phase_turns(a)
                 round_turns(a)
@@ -351,7 +383,8 @@ def tile_gaborbasis_t_kernel(tc, z, mu, K, log_sigma, phi, out):
                 if scalar_copies(i + 1, 0):
                     copy_out(i + 1, 0, True)
                 for j in range(J):
-                    half_square_sum(i + 1, j)
+                    if j > 0 or i + 1 not in GRAM_GROUPS:
+                        half_square_sum(i + 1, j)
             if i + NZ < NG:
                 load(i + NZ)
 

@@ -28,6 +28,7 @@ NXT = 4
 
 SCALAR_COPY_GROUPS = tuple(range(1, NG))
 GRAM_GROUPS = tuple(range(1, 13))
+SCALAR_SECOND_COPY_GROUPS = (1, 2, 4, 5, 7, 8, 10, 11, 13, 14)
 LATE_FROM = 12
 POOL_ARG_GROUPS = (0, 2, 4, 6, 8, 10)
 LOWEST = -3.0e38
@@ -342,7 +343,7 @@ def tile_gaborbasis_t_kernel(tc, z, mu, K, log_sigma, phi, out):
             nc.sync.dma_start(out=o_groups[g], in_=e_all[:, g * GT : (g + 1) * GT])
 
         def scalar_copies(g, j):
-            return j == 0 and g in SCALAR_COPY_GROUPS
+            return (j == 0 and g in SCALAR_COPY_GROUPS) or (j == 1 and g in SCALAR_SECOND_COPY_GROUPS)
 
         def turn_bank(g, j):
             if g > 0 and not scalar_copies(g, j):
@@ -385,6 +386,8 @@ def tile_gaborbasis_t_kernel(tc, z, mu, K, log_sigma, phi, out):
                 for j in range(J):
                     if j > 0 or i + 1 not in GRAM_GROUPS:
                         half_square_sum(i + 1, j)
+                    if j == 1 and scalar_copies(i + 1, 1):
+                        copy_out(i + 1, 1, True)
             if i + NZ < NG:
                 load(i + NZ)
 

@@ -227,36 +227,35 @@ def tile_gaborbasis_t_kernel(tc, z, mu, K, log_sigma, phi, out):
         nc.vector.quantize_mx(out=w_codes[:].bitcast(FP8X4), scales=w_scales[:], in_=gwk[:])
 
         inv_sig_b = inv_sig[:].unsqueeze(1).to_broadcast([P, J, R])
-        phi2_b = phi2[:].unsqueeze(1).to_broadcast([P, J, R])
+        phi2_b = phi2[:].unsqueeze(1).to_broadcast([P, 2, R])
 
         def mx_passes(g):
             codes, scales = q_tiles[g]
-            x_ps = psum.tile([P, BANK], F32, name="x_ps", tag="x%d" % (g % 2))
-            y_ps = psum.tile([P, BANK], F32, name="y_ps", tag="y%d" % (g % 2))
+            lo = psum.tile([P, BANK], F32, name="lo", tag="x%d" % (g % 2))
+            hi = psum.tile([P, BANK], F32, name="hi", tag="y%d" % (g % 2))
+            halves = (lo, hi)
             for j in range(J):
                 for c in range(PASSES):
                     zc = slice((j * PASSES + c) * P, (j * PASSES + c + 1) * P)
-                    for w, acc in ((0, x_ps), (1, y_ps)):
-                        wc = slice((c * 2 + w) * R, (c * 2 + w + 1) * R)
-                        nc.tensor.matmul_mx(
-                            out=acc[:, j * R : (j + 1) * R],
-                            lhsT=codes[:, zc].bitcast(FP8X4),
-                            lhsT_scale=scales[:, zc],
-                            rhs=w_codes[:, wc].bitcast(FP8X4),
-                            rhs_scale=w_scales[:, wc],
-                            start=(c == 0),
-                            stop=(c == PASSES - 1),
-                        )
-            xy_tiles[g] = (x_ps, y_ps)
+                    wc = slice(c * 2 * R, (c + 1) * 2 * R)
+                    nc.tensor.matmul_mx(
+                        out=halves[j // 2][:, j % 2 * 2 * R : (j % 2 + 1) * 2 * R],
+                        lhsT=codes[:, zc].bitcast(FP8X4),
+                        lhsT_scale=scales[:, zc],
+                        rhs=w_codes[:, wc].bitcast(FP8X4),
+                        rhs_scale=w_scales[:, wc],
+                        start=(c == 0),
+                        stop=(c == PASSES - 1),
+                    )
+            xy_tiles[g] = halves
 
         def neg_half_dsq(g):
-            x_ps = xy_tiles[g][0]
             u = work.tile([P, GT], F32, name="u")
             for j in range(J):
                 js = slice(j * R, (j + 1) * R)
                 nc.vector.scalar_tensor_tensor(
                     out=u[:, js],
-                    in0=x_ps[:, js],
+                    in0=xy_tiles[g][j // 2][:, j % 2 * 2 * R : j % 2 * 2 * R + R],
                     scalar=zh[:, g * J + j : g * J + j + 1],
                     in1=muh[:],
                     op0=ALU.subtract,
@@ -292,16 +291,16 @@ def tile_gaborbasis_t_kernel(tc, z, mu, K, log_sigma, phi, out):
             v_tiles[g] = v
 
         def phase_turns(g):
-            y_ps = xy_tiles[g][1]
             w_sb = work.tile([P, GT], F32, name="wv", bufs=NG - LATE_FROM + 1)
-            nc.vector.scalar_tensor_tensor(
-                out=w_sb[:].rearrange("p (j r) -> p j r", j=J),
-                in0=y_ps[:].rearrange("p (j r) -> p j r", j=J),
-                scalar=INV_TWO_PI,
-                in1=phi2_b,
-                op0=ALU.mult,
-                op1=ALU.add,
-            )
+            for h in range(2):
+                nc.vector.scalar_tensor_tensor(
+                    out=w_sb[:, h * 2 * R : (h + 1) * 2 * R].rearrange("p (j r) -> p j r", j=2),
+                    in0=xy_tiles[g][h][:].rearrange("p (j w r) -> p j w r", j=2, w=2)[:, :, 1, :],
+                    scalar=INV_TWO_PI,
+                    in1=phi2_b,
+                    op0=ALU.mult,
+                    op1=ALU.add,
+                )
             w_tiles[g] = w_sb
 
         def round_turns(g):

@@ -28,7 +28,7 @@ NXT = 4
 
 SCALAR_COPY_GROUPS = tuple(range(1, NG))
 GRAM_GROUPS = tuple(range(1, 13))
-SCALAR_SECOND_COPY_GROUPS = (1, 2, 4, 5, 7, 8, 10, 11, 13, 14)
+SCALAR_SECOND_COPY_GROUPS = (2, 5, 8, 11, 14)
 LATE_FROM = 12
 POOL_ARG_GROUPS = (0, 2, 4, 6, 8, 10)
 LOWEST = -3.0e38
@@ -80,9 +80,9 @@ def tile_gaborbasis_t_kernel(tc, z, mu, K, log_sigma, phi, out):
         nc.vector.memset(rows[:], 0.0)
         wk = const.tile([P, 2 * D], BF16, name="wk")
         new_z(0)
+        load_tile(0, 0)
         nc.sync.dma_start(out=rows[0:1, 0:R], in_=log_sigma.unsqueeze(0))
         nc.sync.dma_start(out=rows[0:1, R : 2 * R], in_=phi.unsqueeze(0))
-        load_tile(0, 0)
         load_tile(0, 1)
         nc.sync.dma_start(out=wk[:, 0:D], in_=mu)
         nc.sync.dma_start(out=wk[:, D : 2 * D], in_=K)
@@ -140,7 +140,7 @@ def tile_gaborbasis_t_kernel(tc, z, mu, K, log_sigma, phi, out):
 
         def gram(g):
             gz = grp_tiles[g][:].rearrange("p (j c t w) -> p j c t w", j=J, c=PASSES, w=4)
-            acc = psum.tile([P, BANK], F32, name="xt", tag="xt%d" % (g * J % NXT))
+            acc = psum.tile([P, BANK], F32, name="hi", tag="y%d" % (g % 2))
             for c in range(PASSES):
                 for w in range(4):
                     nc.tensor.matmul(
@@ -171,13 +171,13 @@ def tile_gaborbasis_t_kernel(tc, z, mu, K, log_sigma, phi, out):
             q_tiles[g] = (codes, scales)
 
         new_grp(0)
+        transpose_tile(0, 0)
+        half_square_sum(0, 0)
+        copy_out(0, 0, False)
         pb = psum.tile([P, BANK], F32, name="pb", tag="x0")
         nc.tensor.matmul(pb[:, 0 : 2 * R], lhsT=ones_bf[:], rhs=rows[:], start=True, stop=True)
         bc = const.tile([P, 2 * R], F32, name="bc")
         nc.vector.tensor_copy(out=bc[:], in_=pb[:, 0 : 2 * R])
-        transpose_tile(0, 0)
-        half_square_sum(0, 0)
-        copy_out(0, 0, False)
         inv_sig = const.tile([P, R], F32, name="inv_sig")
         nc.scalar.activation(out=inv_sig[:], in_=bc[:, 0:R], func=ACT.Exp, scale=2.0)
         phi2 = const.tile([P, R], F32, name="phi2")
@@ -212,17 +212,11 @@ def tile_gaborbasis_t_kernel(tc, z, mu, K, log_sigma, phi, out):
             )
             if w == 0:
                 nc.vector.reciprocal(out=inv_sig[:], in_=inv_sig[:])
-        rep = const.tile([P, P], F32, name="rep")
-        nc.vector.tensor_copy(out=rep[:], in_=muh_col[:].to_broadcast([P, P]))
-        pm = psum.tile([P, BANK], F32, name="pm", tag="y0")
-        nc.tensor.transpose(pm[:, 0:P], rep[:], ident[:])
         transpose_tile(0, 2)
         half_square_sum(0, 2)
         transpose_tile(0, 3)
         half_square_sum(0, 3)
         copy_out(0, 2, False)
-        muh = const.tile([P, R], F32, name="muh")
-        nc.vector.tensor_copy(out=muh[:], in_=pm[:, 0:P])
         copy_out(0, 3, False)
         nc.vector.quantize_mx(out=w_codes[:].bitcast(FP8X4), scales=w_scales[:], in_=gwk[:])
 
@@ -350,19 +344,25 @@ def tile_gaborbasis_t_kernel(tc, z, mu, K, log_sigma, phi, out):
             if g + 1 < NG:
                 transpose_tile(g + 1, j)
 
+        rep = const.tile([P, P], F32, name="rep")
+        muh = const.tile([P, R], F32, name="muh")
+        pm = psum.tile([P, BANK], F32, name="pm", tag="y0")
+
         for i in range(NG):
             a = i - 2
             late = a >= LATE_FROM
-            if i in GRAM_GROUPS:
-                gram(i)
             if i >= 1:
                 quantise(i - 1)
-                mx_passes(i - 1)
-            if i in GRAM_GROUPS:
-                gram_diagonal(i)
             if 0 <= a:
                 phase_turns(a)
                 round_turns(a)
+            if i == 1:
+                nc.vector.tensor_copy(out=muh[:], in_=pm[:, 0:P])
+            if i - 1 in GRAM_GROUPS:
+                gram_diagonal(i - 1)
+            if i >= 1:
+                mx_passes(i - 1)
+            if 0 <= a:
                 neg_half_dsq(a)
                 if a in POOL_ARG_GROUPS:
                     pool_clamp(a)
@@ -387,6 +387,11 @@ def tile_gaborbasis_t_kernel(tc, z, mu, K, log_sigma, phi, out):
                         half_square_sum(i + 1, j)
                     if j == 1 and scalar_copies(i + 1, 1):
                         copy_out(i + 1, 1, True)
+            if i in GRAM_GROUPS:
+                gram(i)
+            if i == 0:
+                nc.vector.tensor_copy(out=rep[:], in_=muh_col[:].to_broadcast([P, P]))
+                nc.tensor.transpose(pm[:, 0:P], rep[:], ident[:])
             if i + NZ < NG:
                 load(i + NZ)
 

import math
from contextlib import ExitStack

import concourse.mybir as mybir
from concourse.masks import make_identity

F32 = mybir.dt.float32
BF16 = mybir.dt.bfloat16
I32 = mybir.dt.int32
U32 = mybir.dt.uint32
U8 = mybir.dt.uint8
FP8X4 = mybir.dt.float8_e4m3fn_x4
ALU = mybir.AluOpType
ACT = mybir.ActivationFunctionType

P = 128
R = 128
D = 1024
TOKENS = 8192
J = 4
GT = P * J
NG = TOKENS // GT
PASSES = 2
BANK = 512
WORDS = D // 2
NZ = 5
NXT = 4

SCALAR_COPY_GROUPS = tuple(range(1, NG))
GRAM_GROUPS = tuple(range(1, 13))
SCALAR_SECOND_COPY_GROUPS = (2, 5, 8, 11, 14)
LATE_FROM = 12
POOL_ARG_GROUPS = (0, 2, 4, 6, 8, 10)
LOWEST = -3.0e38
SIN_CHUNKS = ((0, 1), (1, 2), (2, 4), (4, 6), (6, 8), (8, 10), (10, 12), (12, 14), (14, 15), (15, 16))

FLOPS = 2 * 2 * TOKENS * R * D

SQRT_HALF = math.sqrt(0.5)
TWO_PI = 2.0 * math.pi
INV_TWO_PI = 1.0 / TWO_PI
HALF_PI = 0.5 * math.pi


def tile_gaborbasis_t_kernel(tc, z, mu, K, log_sigma, phi, out):
    nc = tc.nc
    z_groups = z.flatten_outer_dims().rearrange("(g p j) k -> g p j k", p=P, j=J)
    o_groups = out.flatten_outer_dims().rearrange("(g p j) r -> g p (j r)", p=P, j=J)

    with ExitStack() as ctx:
        ctx.enter_context(tc.manual_schedule())
        const = ctx.enter_context(tc.tile_pool(name="const", bufs=1))
        zpool = ctx.enter_context(tc.tile_pool(name="zpool", bufs=NZ))
        work = ctx.enter_context(tc.tile_pool(name="work", bufs=2))
        vpool = ctx.enter_context(tc.tile_pool(name="vpool", bufs=4))
        psum = ctx.enter_context(tc.psum_pool(name="psum", bufs=1))

        z_tiles = {}
        xt_tiles = {}
        grp_tiles = {}
        q_tiles = {}
        xy_tiles = {}
        u_tiles = {}
        v_tiles = {}
        w_tiles = {}
        n_tiles = {}
        gram_tiles = {}

        def new_z(g):
            z_tiles[g] = zpool.tile([P, J * D], BF16, name="z_sb")

        def load(g):
            new_z(g)
            nc.sync.dma_start(out=z_tiles[g][:].rearrange("p (j k) -> p j k", j=J), in_=z_groups[g])

        def load_tile(g, j):
            nc.sync.dma_start(out=z_tiles[g][:, j * D : (j + 1) * D], in_=z_groups[g][:, j, :])

        rows = const.tile([P, 2 * R], BF16, name="rows")
        nc.vector.memset(rows[:], 0.0)
        wk = const.tile([P, 2 * D], BF16, name="wk")
        new_z(0)
        load_tile(0, 0)
        nc.sync.dma_start(out=rows[0:1, 0:R], in_=log_sigma.unsqueeze(0))
        nc.sync.dma_start(out=rows[0:1, R : 2 * R], in_=phi.unsqueeze(0))
        load_tile(0, 1)
        nc.sync.dma_start(out=wk[:, 0:D], in_=mu)
        nc.sync.dma_start(out=wk[:, D : 2 * D], in_=K)
        load_tile(0, 2)
        load_tile(0, 3)
        for g in range(1, NZ):
            load(g)

        ones_bf = const.tile([P, P], BF16, name="ones_bf")
        nc.vector.memset(ones_bf[:], 1.0)
        warm = const.tile([P, 2], F32, name="warm")
        nc.vector.memset(warm[:], 0.0)
        nc.scalar.activation(out=warm[:, 1:2], in_=warm[:, 0:1], func=ACT.Exp)
        ident = const.tile([P, P], F32, name="ident")
        make_identity(nc, ident[:])

        zh = const.tile([P, NG * J], F32, name="zh")
        ssum = const.tile([P, NG * J], F32, name="ssum")
        rs = const.tile([P, NG * J], F32, name="rs")
        f_all = const.tile([P, TOKENS], F32, name="f_all")
        e_all = const.tile([P, TOKENS], F32, name="e_all")

        def half_square_sum(g, j):
            junk = work.tile([P, D], BF16, name="junk")
            nc.scalar.activation(
                out=junk[:],
                in_=z_tiles[g][:, j * D : (j + 1) * D],
                func=ACT.Square,
                scale=SQRT_HALF,
                accum_out=zh[:, g * J + j : g * J + j + 1],
            )

        def transpose_tile(g, j):
            z_w = z_tiles[g][:].bitcast(F32)
            t = g * J + j
            xt = psum.tile([P, BANK], F32, name="xt", tag="xt%d" % (t % NXT))
            for cu in range(4):
                nc.tensor.transpose(
                    xt[:, cu * P : (cu + 1) * P],
                    z_w[:, j * WORDS + cu * P : j * WORDS + (cu + 1) * P],
                    ident[:],
                )
            xt_tiles[t] = xt

        def new_grp(g):
            grp_tiles[g] = work.tile([P, J * D], BF16, name="grp", align_bytes=64)

        def copy_out(g, j, on_scalar):
            grp_w = grp_tiles[g][:].bitcast(F32).rearrange("p (j c t u) -> p j c t u", j=J, c=PASSES, u=2)
            src = xt_tiles[g * J + j][:].rearrange("p (c u t) -> p c t u", c=PASSES, u=2)
            if on_scalar:
                nc.scalar.copy(out=grp_w[:, j, :, :, :], in_=src)
            else:
                nc.vector.tensor_copy(out=grp_w[:, j, :, :, :], in_=src)

        def gram(g):
            gz = grp_tiles[g][:].rearrange("p (j c t w) -> p j c t w", j=J, c=PASSES, w=4)
            acc = psum.tile([P, BANK], F32, name="hi", tag="y%d" % (g % 2))
            for c in range(PASSES):
                for w in range(4):
                    nc.tensor.matmul(
                        acc[:, 0:P],
                        lhsT=gz[:, 0, c, :, w],
                        rhs=gz[:, 0, c, :, w],
                        start=(c == 0 and w == 0),
                        stop=(c == PASSES - 1 and w == 3),
                    )
            gram_tiles[g] = acc

        def gram_diagonal(g):
            dj = work.tile([P, P], F32, name="dj")
            nc.vector.scalar_tensor_tensor(
                out=dj[:],
                in0=gram_tiles[g][:, 0:P],
                scalar=0.5,
                in1=ident[:],
                op0=ALU.mult,
                op1=ALU.mult,
                accum_out=zh[:, g * J : g * J + 1],
            )

        def quantise(g):
            codes = work.tile([P, J * PASSES * P], U32, name="codes", align_bytes=64)
            scales = work.tile([P, J * PASSES * P], U8, name="scales", align_bytes=64)
            nc.vector.quantize_mx(out=codes[:].bitcast(FP8X4), scales=scales[:], in_=grp_tiles[g][:])
            q_tiles[g] = (codes, scales)

        new_grp(0)
        transpose_tile(0, 0)
        half_square_sum(0, 0)
        copy_out(0, 0, False)
        pb = psum.tile([P, BANK], F32, name="pb", tag="x0")
        nc.tensor.matmul(pb[:, 0 : 2 * R], lhsT=ones_bf[:], rhs=rows[:], start=True, stop=True)
        bc = const.tile([P, 2 * R], F32, name="bc")
        nc.vector.tensor_copy(out=bc[:], in_=pb[:, 0 : 2 * R])
        inv_sig = const.tile([P, R], F32, name="inv_sig")
        nc.scalar.activation(out=inv_sig[:], in_=bc[:, 0:R], func=ACT.Exp, scale=2.0)
        phi2 = const.tile([P, R], F32, name="phi2")
        nc.vector.tensor_scalar(
            out=phi2[:], in0=bc[:, R : 2 * R], scalar1=HALF_PI, scalar2=INV_TWO_PI, op0=ALU.add, op1=ALU.mult
        )
        transpose_tile(0, 1)
        half_square_sum(0, 1)
        copy_out(0, 1, False)
        nc.vector.tensor_scalar_add(out=inv_sig[:], in0=inv_sig[:], scalar1=1e-8)

        wk_w = wk[:].bitcast(F32)
        gwk = const.tile([P, PASSES * 2 * R * 4], BF16, name="gwk", align_bytes=64)
        gwk_w = gwk[:].bitcast(F32).rearrange("p (c w r u) -> p c w r u", c=PASSES, w=2, u=2)
        w_codes = const.tile([P, PASSES * 2 * R], U32, name="w_codes", align_bytes=64)
        w_scales = const.tile([P, PASSES * 2 * R], U8, name="w_scales", align_bytes=64)
        junk0 = work.tile([P, D], BF16, name="junk")
        muh_col = const.tile([P, 1], F32, name="muh_col")
        nc.scalar.activation(
            out=junk0[:], in_=wk[:, 0:D], func=ACT.Square, scale=SQRT_HALF, accum_out=muh_col[:]
        )
        for w in range(2):
            wt = psum.tile([P, BANK], F32, name="wt", tag="xy"[w] + "1")
            for cu in range(4):
                nc.tensor.transpose(
                    wt[:, cu * P : (cu + 1) * P],
                    wk_w[:, w * WORDS + cu * P : w * WORDS + (cu + 1) * P],
                    ident[:],
                )
            nc.vector.tensor_copy(
                out=gwk_w[:, :, w, :, :], in_=wt[:].rearrange("p (c u r) -> p c r u", c=PASSES, u=2)
            )
            if w == 0:
                nc.vector.reciprocal(out=inv_sig[:], in_=inv_sig[:])
        transpose_tile(0, 2)
        half_square_sum(0, 2)
        transpose_tile(0, 3)
        half_square_sum(0, 3)
        copy_out(0, 2, False)
        copy_out(0, 3, False)
        nc.vector.quantize_mx(out=w_codes[:].bitcast(FP8X4), scales=w_scales[:], in_=gwk[:])

        inv_sig_b = inv_sig[:].unsqueeze(1).to_broadcast([P, J, R])
        phi2_b = phi2[:].unsqueeze(1).to_broadcast([P, 2, R])

        def mx_passes(g):
            codes, scales = q_tiles[g]
            lo = psum.tile([P, BANK], F32, name="lo", tag="x%d" % (g % 2))
            hi = psum.tile([P, BANK], F32, name="hi", tag="y%d" % (g % 2))
            halves = (lo, hi)
            for j in range(J):
                for c in range(PASSES):
                    zc = slice((j * PASSES + c) * P, (j * PASSES + c + 1) * P)
                    wc = slice(c * 2 * R, (c + 1) * 2 * R)
                    nc.tensor.matmul_mx(
                        out=halves[j // 2][:, j % 2 * 2 * R : (j % 2 + 1) * 2 * R],
                        lhsT=codes[:, zc].bitcast(FP8X4),
                        lhsT_scale=scales[:, zc],
                        rhs=w_codes[:, wc].bitcast(FP8X4),
                        rhs_scale=w_scales[:, wc],
                        start=(c == 0),
                        stop=(c == PASSES - 1),
                    )
            xy_tiles[g] = halves

        def neg_half_dsq(g):
            u = work.tile([P, GT], F32, name="u")
            for j in range(J):
                js = slice(j * R, (j + 1) * R)
                nc.vector.scalar_tensor_tensor(
                    out=u[:, js],
                    in0=xy_tiles[g][j // 2][:, j % 2 * 2 * R : j % 2 * 2 * R + R],
                    scalar=zh[:, g * J + j : g * J + j + 1],
                    in1=muh[:],
                    op0=ALU.subtract,
                    op1=ALU.subtract,
                )
            u_tiles[g] = u

        def exp_argument(g):
            v = vpool.tile([P, GT], F32, name="v")
            nc.vector.scalar_tensor_tensor(
                out=v[:].rearrange("p (j r) -> p j r", j=J),
                in0=u_tiles[g][:].rearrange("p (j r) -> p j r", j=J),
                scalar=0.0,
                in1=inv_sig_b,
                op0=ALU.min,
                op1=ALU.mult,
            )
            v_tiles[g] = v

        def pool_clamp(g):
            nc.gpsimd.tensor_scalar(
                out=u_tiles[g][:], in0=u_tiles[g][:], scalar1=0.0, scalar2=LOWEST, op0=ALU.min, op1=ALU.max
            )

        def pool_scale(g):
            v = vpool.tile([P, GT], F32, name="v")
            nc.gpsimd.tensor_tensor(
                out=v[:].rearrange("p (j r) -> p j r", j=J),
                in0=u_tiles[g][:].rearrange("p (j r) -> p j r", j=J),
                in1=inv_sig_b,
                op=ALU.mult,
            )
            v_tiles[g] = v

        def phase_turns(g):
            w_sb = work.tile([P, GT], F32, name="wv", bufs=NG - LATE_FROM + 1)
            for h in range(2):
                nc.vector.scalar_tensor_tensor(
                    out=w_sb[:, h * 2 * R : (h + 1) * 2 * R].rearrange("p (j r) -> p j r", j=2),
                    in0=xy_tiles[g][h][:].rearrange("p (j w r) -> p j w r", j=2, w=2)[:, :, 1, :],
                    scalar=INV_TWO_PI,
                    in1=phi2_b,
                    op0=ALU.mult,
                    op1=ALU.add,
                )
            w_tiles[g] = w_sb

        def round_turns(g):
            n_i = work.tile([P, GT], I32, name="n_i", bufs=NG - LATE_FROM + 1)
            nc.gpsimd.tensor_scalar(out=n_i[:], in0=w_tiles[g][:], scalar1=1.0, scalar2=0.0, op0=ALU.mult, op1=ALU.add)
            n_tiles[g] = n_i

        def reduce_turns(g):
            nc.vector.tensor_tensor(
                out=f_all[:, g * GT : (g + 1) * GT], in0=w_tiles[g][:], in1=n_tiles[g][:], op=ALU.subtract
            )

        def windows(g):
            v = v_tiles[g]
            for j in range(J):
                nc.scalar.activation(
                    out=e_all[:, g * GT + j * R : g * GT + (j + 1) * R],
                    in_=v[:, j * R : (j + 1) * R],
                    func=ACT.Exp,
                    accum_out=ssum[:, g * J + j : g * J + j + 1],
                )

        def sines(g0, g1):
            nc.scalar.activation(
                out=f_all[:, g0 * GT : g1 * GT], in_=f_all[:, g0 * GT : g1 * GT], func=ACT.Sin, scale=TWO_PI
            )

        def product_and_store(g):
            for j in range(J):
                cs = slice(g * GT + j * R, g * GT + (j + 1) * R)
                nc.vector.scalar_tensor_tensor(
                    out=e_all[:, cs],
                    in0=e_all[:, cs],
                    scalar=rs[:, g * J + j : g * J + j + 1],
                    in1=f_all[:, cs],
                    op0=ALU.mult,
                    op1=ALU.mult,
                )
            nc.sync.dma_start(out=o_groups[g], in_=e_all[:, g * GT : (g + 1) * GT])

        def scalar_copies(g, j):
            return (j == 0 and g in SCALAR_COPY_GROUPS) or (j == 1 and g in SCALAR_SECOND_COPY_GROUPS)

        def turn_bank(g, j):
            if g > 0 and not scalar_copies(g, j):
                copy_out(g, j, False)
            if g + 1 < NG:
                transpose_tile(g + 1, j)

        rep = const.tile([P, P], F32, name="rep")
        muh = const.tile([P, R], F32, name="muh")
        pm = psum.tile([P, BANK], F32, name="pm", tag="y0")

        for i in range(NG):
            a = i - 2
            late = a >= LATE_FROM
            if i >= 1:
                quantise(i - 1)
            if 0 <= a:
                phase_turns(a)
                round_turns(a)
            if i == 1:
                nc.vector.tensor_copy(out=muh[:], in_=pm[:, 0:P])
            if i - 1 in GRAM_GROUPS:
                gram_diagonal(i - 1)
            if i >= 1:
                mx_passes(i - 1)
            if 0 <= a:
                neg_half_dsq(a)
                if a in POOL_ARG_GROUPS:
                    pool_clamp(a)
                if a - 1 in POOL_ARG_GROUPS:
                    pool_scale(a - 1)
            if i + 1 < NG:
                new_grp(i + 1)
            if i >= 4:
                windows(i - 4)
            for j in range(J):
                turn_bank(i, j)
            if 0 <= a:
                if a not in POOL_ARG_GROUPS:
                    exp_argument(a)
                if not late:
                    reduce_turns(a)
            if i + 1 < NG:
                if scalar_copies(i + 1, 0):
                    copy_out(i + 1, 0, True)
                for j in range(J):
                    if j > 0 or i + 1 not in GRAM_GROUPS:
                        half_square_sum(i + 1, j)
                    if j == 1 and scalar_copies(i + 1, 1):
                        copy_out(i + 1, 1, True)
            if i in GRAM_GROUPS:
                gram(i)
            if i == 0:
                nc.vector.tensor_copy(out=rep[:], in_=muh_col[:].to_broadcast([P, P]))
                nc.tensor.transpose(pm[:, 0:P], rep[:], ident[:])
            if i + NZ < NG:
                load(i + NZ)

        quantise(NG - 1)
        mx_passes(NG - 1)
        windows(NG - 4)
        windows(NG - 3)
        phase_turns(NG - 2)
        round_turns(NG - 2)
        neg_half_dsq(NG - 2)
        reduce_turns(LATE_FROM)
        exp_argument(NG - 2)
        windows(NG - 2)
        for g in range(LATE_FROM + 1, NG - 2):
            reduce_turns(g)
        neg_half_dsq(NG - 1)
        reduce_turns(NG - 2)
        exp_argument(NG - 1)
        windows(NG - 1)
        phase_turns(NG - 1)
        round_turns(NG - 1)
        nc.vector.tensor_scalar_max(out=rs[:], in0=ssum[:], scalar1=1e-6)
        for g0, g1 in SIN_CHUNKS[:-1]:
            sines(g0, g1)
        nc.vector.reciprocal(out=rs[:], in_=rs[:])
        product_and_store(0)
        reduce_turns(NG - 1)
        for g0, g1 in SIN_CHUNKS[-1:]:
            sines(g0, g1)
        for g in range(1, NG):
            product_and_store(g)
